import numpy as np
import ml_dtypes


def mxq(x, axis, fmt="e4m3"):
    dtype, down = {"e4m3": (ml_dtypes.float8_e4m3fn, 7), "e5m2": (ml_dtypes.float8_e5m2, 14)}[fmt]
    v = np.moveaxis(np.asarray(x, np.float32).astype(ml_dtypes.bfloat16).astype(np.float64), axis, -1)
    blocks = v.reshape(v.shape[:-1] + (-1, 32))
    amax = np.abs(blocks).max(-1, keepdims=True)
    byte = np.maximum(np.where(amax > 0, np.frexp(amax)[1] - 1 + 127, 0) - down, 1)
    scale = np.exp2(byte - 127.0)
    codes = (blocks / scale).astype(np.float32).astype(dtype).astype(np.float64)
    return np.moveaxis((codes * scale).reshape(v.shape), -1, axis)


WIDE = False


def mx_kscale(k):
    if not WIDE:
        return np.ones(k)
    levels = np.array([10, -10, 5, -5, 0])
    if k % 512:
        return np.exp2(np.random.permutation(np.resize(levels, k // 32))).repeat(32)
    a = np.empty((k // 512, 16))
    for p in range(k // 512):
        a[p, :8] = np.random.permutation(np.resize(levels, 8))
        for g in range(8):
            far = levels[np.abs(levels - a[p, g]) >= 10]
            a[p, g + 8] = far[np.random.randint(len(far))]
    return np.exp2(a.ravel()).repeat(32)


BF16 = ml_dtypes.bfloat16


def bf(x):
    return np.asarray(x, np.float32).astype(BF16)


def f64(x):
    return np.asarray(x).astype(np.float64)


B, C, H, W, M, O = 5, 512, 16, 16, 512, 512
N = B * H * W
L2_EPS = 1e-12
BN_EPS = 1e-5


def l2_normalize(x, axis):
    n = np.sqrt(np.sum(x * x, axis=axis, keepdims=True))
    return x / np.maximum(n, L2_EPS)


def setup_inputs():
    s = mx_kscale(C)
    cm = (np.random.standard_normal((N, C)) * 5.0 + np.random.standard_normal((1, C)) * 1.5) / np.sqrt(C)
    w = np.random.standard_normal((O, 2 * C)) * 0.1 / np.sqrt(2 * C)
    w[:, C:] = w[:, C:] / s
    return {"query": bf(np.random.standard_normal((B, C, H, W))), "concat_memory": bf(cm * s), "conv_w": bf(w),
            "bn_gamma": bf(1.0 + 0.1 * np.random.standard_normal(O)), "bn_beta": bf(0.2 * np.random.standard_normal(O))}


def reference(query, concat_memory, conv_w, bn_gamma, bn_beta):
    q_flat = l2_normalize(f64(query), 1).transpose(0, 2, 3, 1).reshape(N, C)
    upd = np.concatenate([q_flat, f64(concat_memory)], axis=1)
    y = mxq(upd, 1, "e4m3") @ mxq(f64(conv_w), 1, "e4m3").T
    y = y.reshape(B, H, W, O).transpose(0, 3, 1, 2)
    mean = np.mean(y, axis=(0, 2, 3), keepdims=True)
    var = np.mean((y - mean) ** 2, axis=(0, 2, 3), keepdims=True)
    y = (y - mean) / np.sqrt(var + BN_EPS)
    y = y * f64(bn_gamma)[None, :, None, None] + f64(bn_beta)[None, :, None, None]
    return np.maximum(y, 0.0)

@@ -1,0 +1,312 @@
+from contextlib import ExitStack
+
+import concourse.mybir as mybir
+from concourse.masks import make_identity
+
+F32 = mybir.dt.float32
+BF16 = mybir.dt.bfloat16
+U32 = mybir.dt.uint32
+U8 = mybir.dt.uint8
+FP8X4 = mybir.dt.float8_e4m3fn_x4
+ACT = mybir.ActivationFunctionType
+ALU = mybir.AluOpType
+
+P = 128
+PACK = 4
+PAIR = 2
+PLANES = PACK // PAIR
+B, C, HW, O = 5, 512, 256, 512
+NPIX = B * HW
+ROW_TILES = HW // P
+OT = O // P
+PASSES = 2
+BANK = 512
+WORDS = C // 2
+BN_STATS = 6
+L2_EPS = 1e-12
+BN_EPS = 1e-5
+FLOPS = 2 * NPIX * 2 * C * O
+CHUNKS = ((0, BANK), (BANK, BANK), (2 * BANK, HW))
+CM_BEHIND_NORM = ((), (), (1,), (2, 3), (4,))
+VECTOR_RELU = ((2, 1), (3, 2))
+
+
+def tile_memory_sup_pb_kernel(tc, query, concat_memory, conv_w, bn_gamma, bn_beta, out):
+    nc = tc.nc
+    with ExitStack() as ctx:
+        keep = ctx.enter_context(tc.tile_pool(name="keep", bufs=1))
+        psum = ctx.enter_context(tc.psum_pool(name="psum", bufs=8))
+        ctx.enter_context(tc.manual_schedule())
+
+        one = keep.tile([P, 1], F32, name="one")
+        nc.vector.memset(one[:], 1.0)
+        bn_eps = keep.tile([P, 1], F32, name="bn_eps")
+        nc.vector.tensor_scalar(out=bn_eps[:], in0=one[:], scalar1=BN_EPS, scalar2=None, op0=ALU.mult)
+        gain_rows = keep.tile([P, P], BF16, name="gain_rows")
+        nc.vector.memset(gain_rows[:], 0.0)
+        ident = keep.tile([P, P], F32, name="ident")
+        make_identity(nc, ident[:])
+        nc.scalar.dma_start(out=gain_rows[0:OT, :], in_=bn_gamma.rearrange("(t p) -> t p", p=P))
+        nc.scalar.dma_start(out=gain_rows[OT : 2 * OT, :], in_=bn_beta.rearrange("(t p) -> t p", p=P))
+        gain_rows_f32 = keep.tile([P, P], F32, name="gain_rows_f32")
+        nc.gpsimd.tensor_copy(out=gain_rows_f32[:], in_=gain_rows[:])
+        table_warm = keep.tile([P, 1], F32, name="table_warm")
+        nc.scalar.activation(out=table_warm[:], in_=one[:], func=ACT.Abs_reciprocal_sqrt)
+
+        q_view = query.rearrange("b (p j) h w -> p b j (h w)", j=PACK)
+        cm_view = concat_memory.rearrange("(r p) c -> p r c", p=P)
+        w_view = conv_w.rearrange("(t p) k -> p t k", p=P)
+        q_raw = [keep.tile([P, PACK, HW], BF16, name="q_raw%d" % b) for b in range(B)]
+        cm_raw = [keep.tile([P, ROW_TILES, C], BF16, name="cm_raw%d" % b) for b in range(B)]
+        w_raw = [keep.tile([P, PASSES * C], BF16, name="w_raw%d" % t) for t in range(OT)]
+
+        def load_q(b):
+            nc.sync.dma_start(out=q_raw[b][:], in_=q_view[:, b, :, :])
+
+        def load_cm(b):
+            nc.sync.dma_start(out=cm_raw[b][:], in_=cm_view[:, ROW_TILES * b : ROW_TILES * (b + 1), :])
+
+        def load_w(t):
+            nc.sync.dma_start(out=w_raw[t][:], in_=w_view[:, t, :])
+
+        load_q(0)
+        load_w(0)
+        load_q(1)
+        load_cm(0)
+        for b in range(2, B):
+            load_q(b)
+        for b in range(1, B):
+            load_cm(b)
+        for t in range(1, OT):
+            load_w(t)
+
+        u_codes = keep.tile([P, PASSES, NPIX], U32, name="u_codes", align_bytes=64)
+        u_scales = keep.tile([P, PASSES, NPIX], U8, name="u_scales", align_bytes=64)
+        w_codes = keep.tile([P, OT, PASSES * P], U32, name="w_codes", align_bytes=64)
+        w_scales = keep.tile([P, OT, PASSES * P], U8, name="w_scales", align_bytes=64)
+        squares = keep.tile([P, PACK, P], BF16, name="squares")
+        q_t, sum_sq, inv_norm, inv_norm_all, q_grouped = {}, {}, {}, {}, {}
+        cm_t, cm_grouped, w_t, w_grouped = {}, {}, {}, {}
+
+        def transpose_q(b):
+            q_t[b] = psum.tile([P, PACK, P], F32, name="q_t%d" % b, tag="bank")
+            words = q_raw[b][:].bitcast(F32)
+            for j in range(PACK):
+                nc.tensor.transpose(q_t[b][:, j, :], words[:, j, :], ident[:])
+
+        def norm_q(b):
+            sum_sq[b] = keep.tile([P, PAIR], F32, name="sum_sq%d" % b)
+            halves = q_t[b][:].bitcast(BF16).rearrange("m j (p e) -> m e j p", e=PAIR)
+            for e in range(PAIR):
+                nc.scalar.activation(
+                    out=squares[:], in_=halves[:, e, :, :], func=ACT.Square, accum_out=sum_sq[b][:, e : e + 1]
+                )
+            inv_norm[b] = keep.tile([P, PAIR], F32, name="inv_norm%d" % b)
+            nc.scalar.activation(out=inv_norm[b][:], in_=sum_sq[b][:], func=ACT.Abs_reciprocal_sqrt)
+
+        def spread_norm(b):
+            inv_norm_all[b] = psum.tile([P, BANK], F32, name="inv_norm_all%d" % b, tag="bank")
+            for e in range(PAIR):
+                nc.tensor.matmul(
+                    out=inv_norm_all[b][:, e:HW:PAIR],
+                    lhsT=inv_norm[b][:, e : e + 1].to_broadcast([P, P]),
+                    rhs=ident[:],
+                    start=True,
+                    stop=True,
+                )
+
+        def normalise_q(b):
+            q_grouped[b] = keep.tile([P, HW, PACK], BF16, name="q_grouped%d" % b, align_bytes=64)
+            nc.vector.scalar_tensor_tensor(
+                out=q_grouped[b][:],
+                in0=inv_norm_all[b][:, 0:HW].unsqueeze(2).to_broadcast([P, HW, PACK]),
+                scalar=1.0 / L2_EPS,
+                in1=q_raw[b][:].rearrange("p j x -> p x j"),
+                op0=ALU.min,
+                op1=ALU.mult,
+            )
+
+        def quantise_q(b):
+            pixels = slice(b * HW, (b + 1) * HW)
+            nc.vector.quantize_mx(
+                out=u_codes[:, 0, pixels].bitcast(FP8X4),
+                scales=u_scales[:, 0, pixels],
+                in_=q_grouped[b][:].rearrange("p x j -> p (x j)"),
+            )
+
+        def transpose_cm(b):
+            cm_t[b] = psum.tile([P, ROW_TILES, PLANES, P], F32, name="cm_t%d" % b, tag="bank")
+            words = cm_raw[b][:].bitcast(F32)
+            for r in range(ROW_TILES):
+                for u in range(PLANES):
+                    nc.tensor.transpose(cm_t[b][:, r, u, :], words[:, r, u:WORDS:PLANES], ident[:])
+
+        def copy_cm(b, copy):
+            cm_grouped[b] = keep.tile([P, ROW_TILES, P, PACK], BF16, name="cm_grouped%d" % b, align_bytes=64)
+            copy(out=cm_grouped[b][:].bitcast(F32), in_=cm_t[b][:].rearrange("p r u v -> p r v u"))
+
+        def quantise_cm(b):
+            pixels = slice(b * HW, (b + 1) * HW)
+            nc.vector.quantize_mx(
+                out=u_codes[:, 1, pixels].bitcast(FP8X4),
+                scales=u_scales[:, 1, pixels],
+                in_=cm_grouped[b][:].rearrange("p r v j -> p (r v j)"),
+            )
+
+        def transpose_w(t):
+            w_t[t] = psum.tile([P, PASSES, PLANES, P], F32, name="w_t%d" % t, tag="bank")
+            words = w_raw[t][:].bitcast(F32)
+            for u in range(PLANES):
+                nc.tensor.transpose(w_t[t][:, 0, u, :], words[:, u:WORDS:PLANES], ident[:])
+            for u in range(PLANES):
+                nc.tensor.transpose(w_t[t][:, 1, u, :], words[:, WORDS + u : 2 * WORDS : PLANES], ident[:])
+
+        def copy_w(t, copy):
+            w_grouped[t] = keep.tile([P, PASSES, P, PACK], BF16, name="w_grouped%d" % t, align_bytes=64)
+            copy(out=w_grouped[t][:].bitcast(F32), in_=w_t[t][:].rearrange("p a u o -> p a o u"))
+
+        def quantise_w(t):
+            nc.vector.quantize_mx(
+                out=w_codes[:, t, :].bitcast(FP8X4),
+                scales=w_scales[:, t, :],
+                in_=w_grouped[t][:].rearrange("p a o j -> p (a o j)"),
+            )
+
+        transpose_q(0)
+        transpose_w(0)
+        transpose_q(1)
+        transpose_cm(0)
+        norm_q(0)
+        copy_w(0, nc.vector.tensor_copy)
+        copy_cm(0, nc.vector.tensor_copy)
+        quantise_w(0)
+        quantise_cm(0)
+        for b in range(B):
+            spread_norm(b)
+            if b + 2 < B:
+                transpose_q(b + 2)
+            for later in CM_BEHIND_NORM[b]:
+                transpose_cm(later)
+            if b + 1 < B:
+                norm_q(b + 1)
+                normalise_q(b)
+                if b >= 1:
+                    quantise_q(b - 1)
+        for t in range(1, OT):
+            transpose_w(t)
+        gain_t = psum.tile([P, BANK], F32, name="gain_t", tag="bank")
+        nc.tensor.transpose(gain_t[:, 0:P], gain_rows_f32[:], ident[:])
+        for b in range(1, B):
+            copy_cm(b, nc.scalar.copy)
+        for t in range(1, OT):
+            copy_w(t, nc.scalar.copy)
+        gain = keep.tile([P, 2 * OT], F32, name="gain")
+        nc.scalar.copy(out=gain[:], in_=gain_t[:, 0 : 2 * OT])
+        neg_gamma = keep.tile([P, OT], F32, name="neg_gamma")
+        nc.scalar.activation(out=neg_gamma[:], in_=gain_t[:, 0:OT], func=ACT.Copy, scale=-1.0)
+        quantise_cm(1)
+        normalise_q(B - 1)
+        quantise_q(B - 2)
+        quantise_cm(2)
+        quantise_cm(3)
+        quantise_q(B - 1)
+        quantise_cm(4)
+        quantise_w(1)
+
+        y, stats, mean_var, rstd, neg_mean_gamma, bn_scale, bn_shift = {}, {}, {}, {}, {}, {}, {}
+
+        def statistics(t):
+            stats[t] = keep.tile([P, len(CHUNKS), BN_STATS], F32, name="stats%d" % t)
+            for i, (first, n) in enumerate(CHUNKS):
+                y[(t, i)] = psum.tile([P, BANK], F32, name="y%d_%d" % (t, i), tag="bank")
+                for a in range(PASSES):
+                    nc.tensor.matmul_mx(
+                        out=y[(t, i)][:, 0:n],
+                        lhsT=w_codes[:, t, a * P : (a + 1) * P].bitcast(FP8X4),
+                        lhsT_scale=w_scales[:, t, a * P : (a + 1) * P],
+                        rhs=u_codes[:, a, first : first + n].bitcast(FP8X4),
+                        rhs_scale=u_scales[:, a, first : first + n],
+                        start=(a == 0),
+                        stop=(a == PASSES - 1),
+                    )
+                nc.vector.bn_stats(out=stats[t][:, i, :], in_=y[(t, i)][:, 0:n])
+
+        def aggregate(t):
+            mean_var[t] = keep.tile([P, 2], F32, name="mean_var%d" % t)
+            nc.vector.bn_aggr(out=mean_var[t][:], in_=stats[t][:].rearrange("p i s -> p (i s)"))
+
+        def chain_first(t):
+            rstd[t] = keep.tile([P, 1], F32, name="rstd%d" % t)
+            nc.scalar.activation(
+                out=rstd[t][:], in_=mean_var[t][:, 1:2], func=ACT.Abs_reciprocal_sqrt, bias=bn_eps[:]
+            )
+            neg_mean_gamma[t] = keep.tile([P, 1], F32, name="neg_mean_gamma%d" % t)
+            nc.scalar.activation(
+                out=neg_mean_gamma[t][:], in_=mean_var[t][:, 0:1], func=ACT.Copy, scale=neg_gamma[:, t : t + 1]
+            )
+
+        def chain_second(t):
+            bn_scale[t] = keep.tile([P, 1], F32, name="bn_scale%d" % t)
+            nc.scalar.activation(out=bn_scale[t][:], in_=rstd[t][:], func=ACT.Copy, scale=gain[:, t : t + 1])
+            bn_shift[t] = keep.tile([P, 1], F32, name="bn_shift%d" % t)
+            nc.scalar.activation(
+                out=bn_shift[t][:],
+                in_=rstd[t][:],
+                func=ACT.Identity,
+                scale=neg_mean_gamma[t][:],
+                bias=gain[:, OT + t : OT + t + 1],
+            )
+
+        def store(t, first, n, result):
+            nc.sync.dma_start(
+                out=out[first // HW : (first + n) // HW, t * P : (t + 1) * P, :, :].rearrange("b p h w -> p b (h w)"),
+                in_=result.rearrange("p (b x) -> p b x", x=HW),
+            )
+
+        def relu_scalar(t, i):
+            first, n = CHUNKS[i]
+            result = keep.tile([P, n], F32, name="result%d_%d" % (t, i))
+            nc.scalar.activation(
+                out=result[:], in_=y[(t, i)][:, 0:n], func=ACT.Relu, bias=bn_shift[t][:], scale=bn_scale[t][:]
+            )
+            store(t, first, n, result[:])
+
+        def relu_vector(t, i):
+            first, n = CHUNKS[i]
+            result = keep.tile([P, n], F32, name="result%d_%d" % (t, i))
+            for x0 in range(0, n, HW):
+                nc.vector.tensor_scalar(
+                    out=result[:, x0 : x0 + HW],
+                    in0=y[(t, i)][:, x0 : x0 + HW],
+                    scalar1=bn_scale[t][:],
+                    scalar2=bn_shift[t][:],
+                    op0=ALU.mult,
+                    op1=ALU.add,
+                )
+            for x0 in range(0, n, HW):
+                nc.vector.tensor_scalar(
+                    out=result[:, x0 : x0 + HW], in0=result[:, x0 : x0 + HW], scalar1=0.0, scalar2=None, op0=ALU.max
+                )
+                store(t, first + x0, HW, result[:, x0 : x0 + HW])
+
+        statistics(0)
+        quantise_w(2)
+        aggregate(0)
+        chain_first(0)
+        chain_second(0)
+        statistics(1)
+        quantise_w(3)
+        aggregate(1)
+        for t in range(OT):
+            for i in range(len(CHUNKS)):
+                if i == len(CHUNKS) - 1 and t + 1 < OT:
+                    chain_first(t + 1)
+                if (t, i) in VECTOR_RELU:
+                    relu_vector(t, i)
+                else:
+                    relu_scalar(t, i)
+            if t + 1 < OT:
+                chain_second(t + 1)
+            if t + 2 < OT:
+                statistics(t + 2)
+                aggregate(t + 2)

@@ -25,6 +25,8 @@ WORDS = C // 2
 BN_STATS = 6
 L2_EPS = 1e-12
 BN_EPS = 1e-5
+GRAM = (1, 2, 3)
+BIG = 2.0**126
 FLOPS = 2 * NPIX * 2 * C * O
 CHUNKS = ((0, BANK), (BANK, BANK), (2 * BANK, HW))
 CM_BEHIND_NORM = ((), (), (1,), (2, 3), (4,))
@@ -46,6 +48,12 @@ def tile_memory_sup_pb_kernel(tc, query, concat_memory, conv_w, bn_gamma, bn_bet
         nc.vector.memset(gain_rows[:], 0.0)
         ident = keep.tile([P, P], F32, name="ident")
         make_identity(nc, ident[:])
+        ident_bf16 = keep.tile([P, P], BF16, name="ident_bf16")
+        nc.vector.tensor_copy(out=ident_bf16[:], in_=ident[:])
+        off_diagonal = keep.tile([P, P], BF16, name="off_diagonal")
+        nc.vector.tensor_scalar(
+            out=off_diagonal[:], in0=ident_bf16[:], scalar1=1.0, scalar2=BIG, op0=ALU.subtract, op1=ALU.mult
+        )
         nc.scalar.dma_start(out=gain_rows[0:OT, :], in_=bn_gamma.rearrange("(t p) -> t p", p=P))
         nc.scalar.dma_start(out=gain_rows[OT : 2 * OT, :], in_=bn_beta.rearrange("(t p) -> t p", p=P))
         gain_rows_f32 = keep.tile([P, P], F32, name="gain_rows_f32")
@@ -84,6 +92,7 @@ def tile_memory_sup_pb_kernel(tc, query, concat_memory, conv_w, bn_gamma, bn_bet
         u_scales = keep.tile([P, PASSES, NPIX], U8, name="u_scales", align_bytes=64)
         w_codes = keep.tile([P, OT, PASSES * P], U32, name="w_codes", align_bytes=64)
         w_scales = keep.tile([P, OT, PASSES * P], U8, name="w_scales", align_bytes=64)
+        gram = {}
         squares = keep.tile([P, PACK, P], BF16, name="squares")
         q_t, sum_sq, inv_norm, inv_norm_all, q_grouped = {}, {}, {}, {}, {}
         cm_t, cm_grouped, w_t, w_grouped = {}, {}, {}, {}
@@ -106,14 +115,42 @@ def tile_memory_sup_pb_kernel(tc, query, concat_memory, conv_w, bn_gamma, bn_bet
 
         def spread_norm(b):
             inv_norm_all[b] = psum.tile([P, BANK], F32, name="inv_norm_all%d" % b, tag="bank")
-            for e in range(PAIR):
-                nc.tensor.matmul(
-                    out=inv_norm_all[b][:, e:HW:PAIR],
-                    lhsT=inv_norm[b][:, e : e + 1].to_broadcast([P, P]),
-                    rhs=ident[:],
-                    start=True,
-                    stop=True,
+            for c in range(2):
+                pixels = slice(c * P, (c + 1) * P) if b in GRAM else slice(c, HW, PAIR)
+                nc.tensor.transpose(
+                    inv_norm_all[b][:, pixels], inv_norm[b][:, c : c + 1].to_broadcast([P, P]), ident[:]
                 )
+
+        def gram_q(b):
+            gram[b] = psum.tile([P, ROW_TILES, P], F32, name="gram%d" % b, tag="bank")
+            for r in range(ROW_TILES):
+                pixels = slice(r * P, (r + 1) * P)
+                for j in range(PACK):
+                    nc.tensor.matmul(
+                        out=gram[b][:, r, :],
+                        lhsT=q_raw[b][:, j, pixels],
+                        rhs=q_raw[b][:, j, pixels],
+                        start=(j == 0),
+                        stop=False,
+                    )
+                nc.tensor.matmul(
+                    out=gram[b][:, r, :], lhsT=ident_bf16[:], rhs=off_diagonal[:], start=False, stop=True
+                )
+
+        def norm_gram(b):
+            sum_sq[b] = keep.tile([P, ROW_TILES], F32, name="sum_sq%d" % b)
+            for r in range(ROW_TILES):
+                nc.scalar.activation(
+                    out=squares[:, r, :], in_=gram[b][:, r, :], func=ACT.Relu, accum_out=sum_sq[b][:, r : r + 1]
+                )
+            inv_norm[b] = keep.tile([P, ROW_TILES], F32, name="inv_norm%d" % b)
+            nc.scalar.activation(out=inv_norm[b][:], in_=sum_sq[b][:], func=ACT.Abs_reciprocal_sqrt)
+
+        def begin_norm(b):
+            (gram_q if b in GRAM else transpose_q)(b)
+
+        def end_norm(b):
+            (norm_gram if b in GRAM else norm_q)(b)
 
         def normalise_q(b):
             q_grouped[b] = keep.tile([P, HW, PACK], BF16, name="q_grouped%d" % b, align_bytes=64)
@@ -172,11 +209,11 @@ def tile_memory_sup_pb_kernel(tc, query, concat_memory, conv_w, bn_gamma, bn_bet
                 in_=w_grouped[t][:].rearrange("p a o j -> p (a o j)"),
             )
 
-        transpose_q(0)
+        begin_norm(0)
         transpose_w(0)
-        transpose_q(1)
+        begin_norm(1)
         transpose_cm(0)
-        norm_q(0)
+        end_norm(0)
         copy_w(0, nc.vector.tensor_copy)
         copy_cm(0, nc.vector.tensor_copy)
         quantise_w(0)
@@ -184,11 +221,11 @@ def tile_memory_sup_pb_kernel(tc, query, concat_memory, conv_w, bn_gamma, bn_bet
         for b in range(B):
             spread_norm(b)
             if b + 2 < B:
-                transpose_q(b + 2)
+                begin_norm(b + 2)
             for later in CM_BEHIND_NORM[b]:
                 transpose_cm(later)
             if b + 1 < B:
-                norm_q(b + 1)
+                end_norm(b + 1)
                 normalise_q(b)
                 if b >= 1:
                     quantise_q(b - 1)

@@ -25,7 +25,7 @@ WORDS = C // 2
 BN_STATS = 6
 L2_EPS = 1e-12
 BN_EPS = 1e-5
-GRAM = (1, 2, 3)
+GRAM = (2, 3)
 BIG = 2.0**126
 FLOPS = 2 * NPIX * 2 * C * O
 CHUNKS = ((0, BANK), (BANK, BANK), (2 * BANK, HW))
@@ -117,8 +117,13 @@ def tile_memory_sup_pb_kernel(tc, query, concat_memory, conv_w, bn_gamma, bn_bet
             inv_norm_all[b] = psum.tile([P, BANK], F32, name="inv_norm_all%d" % b, tag="bank")
             for c in range(2):
                 pixels = slice(c * P, (c + 1) * P) if b in GRAM else slice(c, HW, PAIR)
-                nc.tensor.transpose(
-                    inv_norm_all[b][:, pixels], inv_norm[b][:, c : c + 1].to_broadcast([P, P]), ident[:]
+                nc.tensor.matmul(
+                    out=inv_norm_all[b][:, pixels],
+                    lhsT=inv_norm[b][:, c : c + 1].to_broadcast([P, P]),
+                    rhs=ident[:],
+                    start=True,
+                    stop=True,
+                    is_transpose=(b not in (4,)),
                 )
 
         def gram_q(b):

@@ -27,6 +27,10 @@ L2_EPS = 1e-12
 BN_EPS = 1e-5
 GRAM = (2, 3)
 BIG = 2.0**126
+BANKS = 8
+PREP_BANKS = 6
+ROWS_BANK = 7
+Y_BANKS = (6, 7, 2, 3, 4, 5, 0, 1)
 FLOPS = 2 * NPIX * 2 * C * O
 CHUNKS = ((0, BANK), (BANK, BANK), (2 * BANK, HW))
 CM_BEHIND_NORM = ((), (), (1,), (2, 3), (4,))
@@ -37,13 +41,24 @@ def tile_memory_sup_pb_kernel(tc, query, concat_memory, conv_w, bn_gamma, bn_bet
     nc = tc.nc
     with ExitStack() as ctx:
         keep = ctx.enter_context(tc.tile_pool(name="keep", bufs=1))
-        psum = ctx.enter_context(tc.psum_pool(name="psum", bufs=8))
+        psum = ctx.enter_context(tc.psum_pool(name="psum", bufs=1))
         ctx.enter_context(tc.manual_schedule())
+
+        prepared = []
+
+        def prep_bank(shape, name, dtype=F32):
+            tile = psum.tile(shape, dtype, name=name, tag="bank%d" % (len(prepared) % PREP_BANKS))
+            prepared.append(name)
+            return tile
 
         one = keep.tile([P, 1], F32, name="one")
         nc.vector.memset(one[:], 1.0)
         bn_eps = keep.tile([P, 1], F32, name="bn_eps")
         nc.vector.tensor_scalar(out=bn_eps[:], in0=one[:], scalar1=BN_EPS, scalar2=None, op0=ALU.mult)
+        l2_floor = keep.tile([P, 1], F32, name="l2_floor")
+        nc.vector.tensor_scalar(out=l2_floor[:], in0=one[:], scalar1=L2_EPS * L2_EPS, scalar2=None, op0=ALU.mult)
+        neg_l2_floor = keep.tile([P, 1], F32, name="neg_l2_floor")
+        nc.vector.tensor_scalar(out=neg_l2_floor[:], in0=one[:], scalar1=-L2_EPS * L2_EPS, scalar2=None, op0=ALU.mult)
         gain_rows = keep.tile([P, P], BF16, name="gain_rows")
         nc.vector.memset(gain_rows[:], 0.0)
         ident = keep.tile([P, P], F32, name="ident")
@@ -92,13 +107,20 @@ def tile_memory_sup_pb_kernel(tc, query, concat_memory, conv_w, bn_gamma, bn_bet
         u_scales = keep.tile([P, PASSES, NPIX], U8, name="u_scales", align_bytes=64)
         w_codes = keep.tile([P, OT, PASSES * P], U32, name="w_codes", align_bytes=64)
         w_scales = keep.tile([P, OT, PASSES * P], U8, name="w_scales", align_bytes=64)
-        gram = {}
+        gram, above, q_rows, q_words = {}, {}, {}, {}
         squares = keep.tile([P, PACK, P], BF16, name="squares")
         q_t, sum_sq, inv_norm, inv_norm_all, q_grouped = {}, {}, {}, {}, {}
         cm_t, cm_grouped, w_t, w_grouped = {}, {}, {}, {}
 
+        warm = prep_bank([P, BANK], "warm")
+        for i in range(3):
+            nc.tensor.matmul(out=warm[:, 0:P], lhsT=ident[:], rhs=ident[:], start=True, stop=True)
+
         def transpose_q(b):
-            q_t[b] = psum.tile([P, PACK, P], F32, name="q_t%d" % b, tag="bank")
+            if b == B - 1:
+                q_t[b] = psum.tile([P, PACK, P], F32, name="q_t%d" % b, tag="bank%d" % ROWS_BANK)
+            else:
+                q_t[b] = prep_bank([P, PACK, P], "q_t%d" % b)
             words = q_raw[b][:].bitcast(F32)
             for j in range(PACK):
                 nc.tensor.transpose(q_t[b][:, j, :], words[:, j, :], ident[:])
@@ -114,7 +136,7 @@ def tile_memory_sup_pb_kernel(tc, query, concat_memory, conv_w, bn_gamma, bn_bet
             nc.scalar.activation(out=inv_norm[b][:], in_=sum_sq[b][:], func=ACT.Abs_reciprocal_sqrt)
 
         def spread_norm(b):
-            inv_norm_all[b] = psum.tile([P, BANK], F32, name="inv_norm_all%d" % b, tag="bank")
+            inv_norm_all[b] = prep_bank([P, BANK], "inv_norm_all%d" % b)
             for c in range(2):
                 pixels = slice(c * P, (c + 1) * P) if b in GRAM else slice(c, HW, PAIR)
                 nc.tensor.matmul(
@@ -123,11 +145,11 @@ def tile_memory_sup_pb_kernel(tc, query, concat_memory, conv_w, bn_gamma, bn_bet
                     rhs=ident[:],
                     start=True,
                     stop=True,
-                    is_transpose=(b not in (4,)),
+                    is_transpose=(b not in (3,)),
                 )
 
         def gram_q(b):
-            gram[b] = psum.tile([P, ROW_TILES, P], F32, name="gram%d" % b, tag="bank")
+            gram[b] = prep_bank([P, ROW_TILES, P], "gram%d" % b)
             for r in range(ROW_TILES):
                 pixels = slice(r * P, (r + 1) * P)
                 for j in range(PACK):
@@ -150,6 +172,47 @@ def tile_memory_sup_pb_kernel(tc, query, concat_memory, conv_w, bn_gamma, bn_bet
                 )
             inv_norm[b] = keep.tile([P, ROW_TILES], F32, name="inv_norm%d" % b)
             nc.scalar.activation(out=inv_norm[b][:], in_=sum_sq[b][:], func=ACT.Abs_reciprocal_sqrt)
+
+        def norm_rows(b):
+            sum_sq[b] = keep.tile([P, PAIR], F32, name="sum_sq%d" % b)
+            halves = q_t[b][:].bitcast(BF16).rearrange("m j (p e) -> m e j p", e=PAIR)
+            for e in range(PAIR):
+                nc.scalar.activation(
+                    out=squares[:], in_=halves[:, e, :, :], func=ACT.Square, accum_out=sum_sq[b][:, e : e + 1]
+                )
+
+        def clamp_rows(b):
+            above[b] = keep.tile([P, PAIR], F32, name="above%d" % b)
+            nc.scalar.activation(out=above[b][:], in_=sum_sq[b][:], func=ACT.Relu, bias=neg_l2_floor[:])
+
+        def root_rows(b):
+            inv_norm[b] = keep.tile([P, PAIR], F32, name="inv_norm%d" % b)
+            nc.scalar.activation(out=inv_norm[b][:], in_=above[b][:], func=ACT.Abs_reciprocal_sqrt, bias=l2_floor[:])
+
+        def scale_rows(b):
+            q_rows[b] = keep.tile([P, PAIR, C], BF16, name="q_rows%d" % b)
+            halves = q_t[b][:].bitcast(BF16).rearrange("m j (p e) -> m e p j", e=PAIR)
+            for e in range(PAIR):
+                nc.scalar.activation(
+                    out=q_rows[b][:, e, :].rearrange("m (p j) -> m p j", j=PACK),
+                    in_=halves[:, e, :, :],
+                    func=ACT.Copy,
+                    scale=inv_norm[b][:, e : e + 1],
+                )
+
+        def transpose_rows(b):
+            q_words[b] = prep_bank([P, PAIR, PLANES, P], "q_words%d" % b)
+            words = q_rows[b][:].bitcast(F32)
+            for e in range(PAIR):
+                for u in range(PLANES):
+                    nc.tensor.transpose(q_words[b][:, e, u, :], words[:, e, u:WORDS:PLANES], ident[:])
+
+        def copy_rows(b, copy):
+            q_grouped[b] = keep.tile([P, HW, PACK], BF16, name="q_grouped%d" % b, align_bytes=64)
+            copy(
+                out=q_grouped[b][:].bitcast(F32).rearrange("p (m e) u -> p m e u", e=PAIR),
+                in_=q_words[b][:].rearrange("p e u m -> p m e u"),
+            )
 
         def begin_norm(b):
             (gram_q if b in GRAM else transpose_q)(b)
@@ -177,7 +240,7 @@ def tile_memory_sup_pb_kernel(tc, query, concat_memory, conv_w, bn_gamma, bn_bet
             )
 
         def transpose_cm(b):
-            cm_t[b] = psum.tile([P, ROW_TILES, PLANES, P], F32, name="cm_t%d" % b, tag="bank")
+            cm_t[b] = prep_bank([P, ROW_TILES, PLANES, P], "cm_t%d" % b)
             words = cm_raw[b][:].bitcast(F32)
             for r in range(ROW_TILES):
                 for u in range(PLANES):
@@ -196,7 +259,7 @@ def tile_memory_sup_pb_kernel(tc, query, concat_memory, conv_w, bn_gamma, bn_bet
             )
 
         def transpose_w(t):
-            w_t[t] = psum.tile([P, PASSES, PLANES, P], F32, name="w_t%d" % t, tag="bank")
+            w_t[t] = prep_bank([P, PASSES, PLANES, P], "w_t%d" % t)
             words = w_raw[t][:].bitcast(F32)
             for u in range(PLANES):
                 nc.tensor.transpose(w_t[t][:, 0, u, :], words[:, u:WORDS:PLANES], ident[:])
@@ -214,64 +277,32 @@ def tile_memory_sup_pb_kernel(tc, query, concat_memory, conv_w, bn_gamma, bn_bet
                 in_=w_grouped[t][:].rearrange("p a o j -> p (a o j)"),
             )
 
-        begin_norm(0)
-        transpose_w(0)
-        begin_norm(1)
-        transpose_cm(0)
-        end_norm(0)
-        copy_w(0, nc.vector.tensor_copy)
-        copy_cm(0, nc.vector.tensor_copy)
-        quantise_w(0)
-        quantise_cm(0)
-        for b in range(B):
-            spread_norm(b)
-            if b + 2 < B:
-                begin_norm(b + 2)
-            for later in CM_BEHIND_NORM[b]:
-                transpose_cm(later)
-            if b + 1 < B:
-                end_norm(b + 1)
-                normalise_q(b)
-                if b >= 1:
-                    quantise_q(b - 1)
-        for t in range(1, OT):
-            transpose_w(t)
-        gain_t = psum.tile([P, BANK], F32, name="gain_t", tag="bank")
-        nc.tensor.transpose(gain_t[:, 0:P], gain_rows_f32[:], ident[:])
-        for b in range(1, B):
-            copy_cm(b, nc.scalar.copy)
-        for t in range(1, OT):
-            copy_w(t, nc.scalar.copy)
-        gain = keep.tile([P, 2 * OT], F32, name="gain")
-        nc.scalar.copy(out=gain[:], in_=gain_t[:, 0 : 2 * OT])
-        neg_gamma = keep.tile([P, OT], F32, name="neg_gamma")
-        nc.scalar.activation(out=neg_gamma[:], in_=gain_t[:, 0:OT], func=ACT.Copy, scale=-1.0)
-        quantise_cm(1)
-        normalise_q(B - 1)
-        quantise_q(B - 2)
-        quantise_cm(2)
-        quantise_cm(3)
-        quantise_q(B - 1)
-        quantise_cm(4)
-        quantise_w(1)
-
         y, stats, mean_var, rstd, neg_mean_gamma, bn_scale, bn_shift = {}, {}, {}, {}, {}, {}, {}
 
+        def multiply(t, i):
+            first, n = CHUNKS[i]
+            bank = Y_BANKS[(len(CHUNKS) * t + i) % BANKS]
+            y[(t, i)] = psum.tile([P, BANK], F32, name="y%d_%d" % (t, i), tag="bank%d" % bank)
+            for a in range(PASSES):
+                nc.tensor.matmul_mx(
+                    out=y[(t, i)][:, 0:n],
+                    lhsT=w_codes[:, t, a * P : (a + 1) * P].bitcast(FP8X4),
+                    lhsT_scale=w_scales[:, t, a * P : (a + 1) * P],
+                    rhs=u_codes[:, a, first : first + n].bitcast(FP8X4),
+                    rhs_scale=u_scales[:, a, first : first + n],
+                    start=(a == 0),
+                    stop=(a == PASSES - 1),
+                )
+
+        def chunk_statistics(t, i):
+            if i == 0:
+                stats[t] = keep.tile([P, len(CHUNKS), BN_STATS], F32, name="stats%d" % t)
+            nc.vector.bn_stats(out=stats[t][:, i, :], in_=y[(t, i)][:, 0 : CHUNKS[i][1]])
+
         def statistics(t):
-            stats[t] = keep.tile([P, len(CHUNKS), BN_STATS], F32, name="stats%d" % t)
-            for i, (first, n) in enumerate(CHUNKS):
-                y[(t, i)] = psum.tile([P, BANK], F32, name="y%d_%d" % (t, i), tag="bank")
-                for a in range(PASSES):
-                    nc.tensor.matmul_mx(
-                        out=y[(t, i)][:, 0:n],
-                        lhsT=w_codes[:, t, a * P : (a + 1) * P].bitcast(FP8X4),
-                        lhsT_scale=w_scales[:, t, a * P : (a + 1) * P],
-                        rhs=u_codes[:, a, first : first + n].bitcast(FP8X4),
-                        rhs_scale=u_scales[:, a, first : first + n],
-                        start=(a == 0),
-                        stop=(a == PASSES - 1),
-                    )
-                nc.vector.bn_stats(out=stats[t][:, i, :], in_=y[(t, i)][:, 0:n])
+            for i in range(len(CHUNKS)):
+                multiply(t, i)
+                chunk_statistics(t, i)
 
         def aggregate(t):
             mean_var[t] = keep.tile([P, 2], F32, name="mean_var%d" % t)
@@ -331,9 +362,73 @@ def tile_memory_sup_pb_kernel(tc, query, concat_memory, conv_w, bn_gamma, bn_bet
                 )
                 store(t, first + x0, HW, result[:, x0 : x0 + HW])
 
-        statistics(0)
+        transpose_q(0)
+        transpose_w(0)
+        transpose_q(1)
+        transpose_cm(0)
+        norm_q(0)
+        copy_w(0, nc.vector.tensor_copy)
+        copy_cm(0, nc.vector.tensor_copy)
+        norm_q(1)
+        gram_q(2)
+        quantise_w(0)
+        spread_norm(0)
+        transpose_q(4)
+        normalise_q(0)
+        quantise_cm(0)
+        norm_gram(2)
+        transpose_cm(1)
+        spread_norm(1)
+        norm_rows(4)
+        normalise_q(1)
+        quantise_q(0)
+        spread_norm(2)
+        gram_q(3)
+        normalise_q(2)
+        norm_gram(3)
+        transpose_cm(2)
+        copy_cm(1, nc.scalar.copy)
+        clamp_rows(4)
+        transpose_cm(3)
+        spread_norm(3)
+        copy_cm(2, nc.scalar.copy)
+        root_rows(4)
+        quantise_q(1)
+        quantise_cm(1)
+        quantise_q(2)
+        normalise_q(3)
+        transpose_cm(4)
+        gain_t = prep_bank([P, BANK], "gain_t")
+        nc.tensor.transpose(gain_t[:, 0:P], gain_rows_f32[:], ident[:])
+        transpose_w(1)
+        scale_rows(4)
+        copy_cm(3, nc.scalar.copy)
+        copy_cm(4, nc.scalar.copy)
+        transpose_rows(4)
+        multiply(0, 0)
+        quantise_cm(2)
+        quantise_q(3)
+        quantise_cm(3)
+        quantise_cm(4)
+        multiply(0, 1)
+        transpose_w(2)
+        copy_rows(4, nc.scalar.copy)
+        quantise_q(4)
+        multiply(0, 2)
+        transpose_w(3)
+        chunk_statistics(0, 0)
+        copy_w(1, nc.scalar.copy)
+        gain = keep.tile([P, 2 * OT], F32, name="gain")
+        nc.scalar.copy(out=gain[:], in_=gain_t[:, 0 : 2 * OT])
+        neg_gamma = keep.tile([P, OT], F32, name="neg_gamma")
+        nc.scalar.activation(out=neg_gamma[:], in_=gain_t[:, 0:OT], func=ACT.Copy, scale=-1.0)
+        copy_w(2, nc.scalar.copy)
+        quantise_w(1)
+        chunk_statistics(0, 1)
+        chunk_statistics(0, 2)
         quantise_w(2)
         aggregate(0)
+        copy_w(3, nc.scalar.copy)
         chain_first(0)
         chain_second(0)
         statistics(1)

@@ -69,10 +69,6 @@ def tile_memory_sup_pb_kernel(tc, query, concat_memory, conv_w, bn_gamma, bn_bet
         nc.vector.tensor_scalar(
             out=off_diagonal[:], in0=ident_bf16[:], scalar1=1.0, scalar2=BIG, op0=ALU.subtract, op1=ALU.mult
         )
-        nc.scalar.dma_start(out=gain_rows[0:OT, :], in_=bn_gamma.rearrange("(t p) -> t p", p=P))
-        nc.scalar.dma_start(out=gain_rows[OT : 2 * OT, :], in_=bn_beta.rearrange("(t p) -> t p", p=P))
-        gain_rows_f32 = keep.tile([P, P], F32, name="gain_rows_f32")
-        nc.gpsimd.tensor_copy(out=gain_rows_f32[:], in_=gain_rows[:])
         table_warm = keep.tile([P, 1], F32, name="table_warm")
         nc.scalar.activation(out=table_warm[:], in_=one[:], func=ACT.Abs_reciprocal_sqrt)
 
@@ -96,12 +92,18 @@ def tile_memory_sup_pb_kernel(tc, query, concat_memory, conv_w, bn_gamma, bn_bet
         load_w(0)
         load_q(1)
         load_cm(0)
+        load_q(2)
+        load_q(4)
+        load_cm(1)
+        load_q(3)
         for b in range(2, B):
-            load_q(b)
-        for b in range(1, B):
             load_cm(b)
         for t in range(1, OT):
             load_w(t)
+        nc.sync.dma_start(out=gain_rows[0:OT, :], in_=bn_gamma.rearrange("(t p) -> t p", p=P))
+        nc.sync.dma_start(out=gain_rows[OT : 2 * OT, :], in_=bn_beta.rearrange("(t p) -> t p", p=P))
+        gain_rows_f32 = keep.tile([P, P], F32, name="gain_rows_f32")
+        nc.gpsimd.tensor_copy(out=gain_rows_f32[:], in_=gain_rows[:])
 
         u_codes = keep.tile([P, PASSES, NPIX], U32, name="u_codes", align_bytes=64)
         u_scales = keep.tile([P, PASSES, NPIX], U8, name="u_scales", align_bytes=64)

@@ -102,8 +102,6 @@ def tile_memory_sup_pb_kernel(tc, query, concat_memory, conv_w, bn_gamma, bn_bet
             load_w(t)
         nc.sync.dma_start(out=gain_rows[0:OT, :], in_=bn_gamma.rearrange("(t p) -> t p", p=P))
         nc.sync.dma_start(out=gain_rows[OT : 2 * OT, :], in_=bn_beta.rearrange("(t p) -> t p", p=P))
-        gain_rows_f32 = keep.tile([P, P], F32, name="gain_rows_f32")
-        nc.gpsimd.tensor_copy(out=gain_rows_f32[:], in_=gain_rows[:])
 
         u_codes = keep.tile([P, PASSES, NPIX], U32, name="u_codes", align_bytes=64)
         u_scales = keep.tile([P, PASSES, NPIX], U8, name="u_scales", align_bytes=64)
@@ -147,7 +145,7 @@ def tile_memory_sup_pb_kernel(tc, query, concat_memory, conv_w, bn_gamma, bn_bet
                     rhs=ident[:],
                     start=True,
                     stop=True,
-                    is_transpose=(b not in (3,)),
+                    is_transpose=(b not in (0, 3)),
                 )
 
         def gram_q(b):
@@ -400,8 +398,8 @@ def tile_memory_sup_pb_kernel(tc, query, concat_memory, conv_w, bn_gamma, bn_bet
         quantise_q(2)
         normalise_q(3)
         transpose_cm(4)
-        gain_t = prep_bank([P, BANK], "gain_t")
-        nc.tensor.transpose(gain_t[:, 0:P], gain_rows_f32[:], ident[:])
+        gain_t = prep_bank([P, 2 * BANK], "gain_t", BF16)
+        nc.tensor.transpose(gain_t[:, 0:P], gain_rows[:], ident_bf16[:])
         transpose_w(1)
         scale_rows(4)
         copy_cm(3, nc.scalar.copy)

@@ -31,6 +31,7 @@ BANKS = 8
 PREP_BANKS = 6
 ROWS_BANK = 7
 Y_BANKS = (6, 7, 2, 3, 4, 5, 0, 1)
+RUN = 4
 FLOPS = 2 * NPIX * 2 * C * O
 CHUNKS = ((0, BANK), (BANK, BANK), (2 * BANK, HW))
 CM_BEHIND_NORM = ((), (), (1,), (2, 3), (4,))
@@ -132,8 +133,14 @@ def tile_memory_sup_pb_kernel(tc, query, concat_memory, conv_w, bn_gamma, bn_bet
                 nc.scalar.activation(
                     out=squares[:], in_=halves[:, e, :, :], func=ACT.Square, accum_out=sum_sq[b][:, e : e + 1]
                 )
+
+        def clamp_q(b):
+            above[b] = keep.tile([P, PAIR], F32, name="above%d" % b)
+            nc.scalar.activation(out=above[b][:], in_=sum_sq[b][:], func=ACT.Relu, bias=neg_l2_floor[:])
+
+        def root_q(b):
             inv_norm[b] = keep.tile([P, PAIR], F32, name="inv_norm%d" % b)
-            nc.scalar.activation(out=inv_norm[b][:], in_=sum_sq[b][:], func=ACT.Abs_reciprocal_sqrt)
+            nc.scalar.activation(out=inv_norm[b][:], in_=above[b][:], func=ACT.Abs_reciprocal_sqrt, bias=l2_floor[:])
 
         def spread_norm(b):
             inv_norm_all[b] = prep_bank([P, BANK], "inv_norm_all%d" % b)
@@ -165,29 +172,15 @@ def tile_memory_sup_pb_kernel(tc, query, concat_memory, conv_w, bn_gamma, bn_bet
                 )
 
         def norm_gram(b):
-            sum_sq[b] = keep.tile([P, ROW_TILES], F32, name="sum_sq%d" % b)
+            above[b] = keep.tile([P, ROW_TILES], F32, name="above%d" % b)
             for r in range(ROW_TILES):
                 nc.scalar.activation(
-                    out=squares[:, r, :], in_=gram[b][:, r, :], func=ACT.Relu, accum_out=sum_sq[b][:, r : r + 1]
+                    out=squares[:, r, :],
+                    in_=gram[b][:, r, :],
+                    func=ACT.Relu,
+                    bias=neg_l2_floor[:],
+                    accum_out=above[b][:, r : r + 1],
                 )
-            inv_norm[b] = keep.tile([P, ROW_TILES], F32, name="inv_norm%d" % b)
-            nc.scalar.activation(out=inv_norm[b][:], in_=sum_sq[b][:], func=ACT.Abs_reciprocal_sqrt)
-
-        def norm_rows(b):
-            sum_sq[b] = keep.tile([P, PAIR], F32, name="sum_sq%d" % b)
-            halves = q_t[b][:].bitcast(BF16).rearrange("m j (p e) -> m e j p", e=PAIR)
-            for e in range(PAIR):
-                nc.scalar.activation(
-                    out=squares[:], in_=halves[:, e, :, :], func=ACT.Square, accum_out=sum_sq[b][:, e : e + 1]
-                )
-
-        def clamp_rows(b):
-            above[b] = keep.tile([P, PAIR], F32, name="above%d" % b)
-            nc.scalar.activation(out=above[b][:], in_=sum_sq[b][:], func=ACT.Relu, bias=neg_l2_floor[:])
-
-        def root_rows(b):
-            inv_norm[b] = keep.tile([P, PAIR], F32, name="inv_norm%d" % b)
-            nc.scalar.activation(out=inv_norm[b][:], in_=above[b][:], func=ACT.Abs_reciprocal_sqrt, bias=l2_floor[:])
 
         def scale_rows(b):
             q_rows[b] = keep.tile([P, PAIR, C], BF16, name="q_rows%d" % b)
@@ -214,21 +207,16 @@ def tile_memory_sup_pb_kernel(tc, query, concat_memory, conv_w, bn_gamma, bn_bet
                 in_=q_words[b][:].rearrange("p e u m -> p m e u"),
             )
 
-        def begin_norm(b):
-            (gram_q if b in GRAM else transpose_q)(b)
-
-        def end_norm(b):
-            (norm_gram if b in GRAM else norm_q)(b)
-
         def normalise_q(b):
             q_grouped[b] = keep.tile([P, HW, PACK], BF16, name="q_grouped%d" % b, align_bytes=64)
-            nc.vector.scalar_tensor_tensor(
-                out=q_grouped[b][:],
-                in0=inv_norm_all[b][:, 0:HW].unsqueeze(2).to_broadcast([P, HW, PACK]),
-                scalar=1.0 / L2_EPS,
-                in1=q_raw[b][:].rearrange("p j x -> p x j"),
-                op0=ALU.min,
-                op1=ALU.mult,
+            nc.vector.tensor_tensor(
+                out=q_grouped[b][:].rearrange("p (c i) j -> p c j i", i=RUN),
+                in0=inv_norm_all[b][:, 0:HW]
+                .rearrange("p (c i) -> p c i", i=RUN)
+                .unsqueeze(2)
+                .to_broadcast([P, HW // RUN, PACK, RUN]),
+                in1=q_raw[b][:].rearrange("p j (c i) -> p c j i", i=RUN),
+                op=ALU.mult,
             )
 
         def quantise_q(b):
@@ -367,6 +355,8 @@ def tile_memory_sup_pb_kernel(tc, query, concat_memory, conv_w, bn_gamma, bn_bet
         transpose_q(1)
         transpose_cm(0)
         norm_q(0)
+        clamp_q(0)
+        root_q(0)
         copy_w(0, nc.vector.tensor_copy)
         copy_cm(0, nc.vector.tensor_copy)
         norm_q(1)
@@ -377,22 +367,26 @@ def tile_memory_sup_pb_kernel(tc, query, concat_memory, conv_w, bn_gamma, bn_bet
         normalise_q(0)
         quantise_cm(0)
         norm_gram(2)
+        clamp_q(1)
+        root_q(2)
+        root_q(1)
         transpose_cm(1)
         spread_norm(1)
-        norm_rows(4)
+        norm_q(4)
         normalise_q(1)
         quantise_q(0)
         spread_norm(2)
         gram_q(3)
         normalise_q(2)
         norm_gram(3)
+        clamp_q(4)
+        root_q(3)
         transpose_cm(2)
         copy_cm(1, nc.scalar.copy)
-        clamp_rows(4)
         transpose_cm(3)
         spread_norm(3)
         copy_cm(2, nc.scalar.copy)
-        root_rows(4)
+        root_q(4)
         quantise_q(1)
         quantise_cm(1)
         quantise_q(2)
@@ -412,10 +406,10 @@ def tile_memory_sup_pb_kernel(tc, query, concat_memory, conv_w, bn_gamma, bn_bet
         quantise_cm(4)
         multiply(0, 1)
         transpose_w(2)
+        transpose_w(3)
         copy_rows(4, nc.scalar.copy)
         quantise_q(4)
         multiply(0, 2)
-        transpose_w(3)
         chunk_statistics(0, 0)
         copy_w(1, nc.scalar.copy)
         gain = keep.tile([P, 2 * OT], F32, name="gain")

@@ -187,8 +187,8 @@ def tile_memory_sup_pb_kernel(tc, query, concat_memory, conv_w, bn_gamma, bn_bet
             halves = q_t[b][:].bitcast(BF16).rearrange("m j (p e) -> m e p j", e=PAIR)
             for e in range(PAIR):
                 nc.scalar.activation(
-                    out=q_rows[b][:, e, :].rearrange("m (p j) -> m p j", j=PACK),
-                    in_=halves[:, e, :, :],
+                    out=q_rows[b][:, e, :].rearrange("m (c i j) -> m c j i", i=RUN, j=PACK),
+                    in_=halves[:, e, :, :].rearrange("m (c i) j -> m c j i", i=RUN),
                     func=ACT.Copy,
                     scale=inv_norm[b][:, e : e + 1],
                 )
@@ -378,15 +378,15 @@ def tile_memory_sup_pb_kernel(tc, query, concat_memory, conv_w, bn_gamma, bn_bet
         spread_norm(2)
         gram_q(3)
         normalise_q(2)
+        copy_cm(1, nc.scalar.copy)
         norm_gram(3)
         clamp_q(4)
         root_q(3)
+        root_q(4)
         transpose_cm(2)
-        copy_cm(1, nc.scalar.copy)
         transpose_cm(3)
         spread_norm(3)
         copy_cm(2, nc.scalar.copy)
-        root_q(4)
         quantise_q(1)
         quantise_cm(1)
         quantise_q(2)

from contextlib import ExitStack

import concourse.mybir as mybir
from concourse.masks import make_identity

F32 = mybir.dt.float32
BF16 = mybir.dt.bfloat16
U32 = mybir.dt.uint32
U8 = mybir.dt.uint8
FP8X4 = mybir.dt.float8_e4m3fn_x4
ACT = mybir.ActivationFunctionType
ALU = mybir.AluOpType

P = 128
PACK = 4
PAIR = 2
PLANES = PACK // PAIR
B, C, HW, O = 5, 512, 256, 512
NPIX = B * HW
ROW_TILES = HW // P
OT = O // P
PASSES = 2
BANK = 512
WORDS = C // 2
BN_STATS = 6
L2_EPS = 1e-12
BN_EPS = 1e-5
GRAM = (2, 3)
BIG = 2.0**126
BANKS = 8
PREP_BANKS = 6
ROWS_BANK = 7
Y_BANKS = (6, 7, 2, 3, 4, 5, 0, 1)
RUN = 4
FLOPS = 2 * NPIX * 2 * C * O
CHUNKS = ((0, BANK), (BANK, BANK), (2 * BANK, HW))
CM_BEHIND_NORM = ((), (), (1,), (2, 3), (4,))
VECTOR_RELU = ((2, 1), (3, 2))


def tile_memory_sup_pb_kernel(tc, query, concat_memory, conv_w, bn_gamma, bn_beta, out):
    nc = tc.nc
    with ExitStack() as ctx:
        keep = ctx.enter_context(tc.tile_pool(name="keep", bufs=1))
        psum = ctx.enter_context(tc.psum_pool(name="psum", bufs=1))
        ctx.enter_context(tc.manual_schedule())

        prepared = []

        def prep_bank(shape, name, dtype=F32):
            tile = psum.tile(shape, dtype, name=name, tag="bank%d" % (len(prepared) % PREP_BANKS))
            prepared.append(name)
            return tile

        one = keep.tile([P, 1], F32, name="one")
        nc.vector.memset(one[:], 1.0)
        bn_eps = keep.tile([P, 1], F32, name="bn_eps")
        nc.vector.tensor_scalar(out=bn_eps[:], in0=one[:], scalar1=BN_EPS, scalar2=None, op0=ALU.mult)
        l2_floor = keep.tile([P, 1], F32, name="l2_floor")
        nc.vector.tensor_scalar(out=l2_floor[:], in0=one[:], scalar1=L2_EPS * L2_EPS, scalar2=None, op0=ALU.mult)
        neg_l2_floor = keep.tile([P, 1], F32, name="neg_l2_floor")
        nc.vector.tensor_scalar(out=neg_l2_floor[:], in0=one[:], scalar1=-L2_EPS * L2_EPS, scalar2=None, op0=ALU.mult)
        gain_rows = keep.tile([P, P], BF16, name="gain_rows")
        nc.vector.memset(gain_rows[:], 0.0)
        ident = keep.tile([P, P], F32, name="ident")
        make_identity(nc, ident[:])
        ident_bf16 = keep.tile([P, P], BF16, name="ident_bf16")
        nc.vector.tensor_copy(out=ident_bf16[:], in_=ident[:])
        off_diagonal = keep.tile([P, P], BF16, name="off_diagonal")
        nc.vector.tensor_scalar(
            out=off_diagonal[:], in0=ident_bf16[:], scalar1=1.0, scalar2=BIG, op0=ALU.subtract, op1=ALU.mult
        )
        table_warm = keep.tile([P, 1], F32, name="table_warm")
        nc.scalar.activation(out=table_warm[:], in_=one[:], func=ACT.Abs_reciprocal_sqrt)

        q_view = query.rearrange("b (p j) h w -> p b j (h w)", j=PACK)
        cm_view = concat_memory.rearrange("(r p) c -> p r c", p=P)
        w_view = conv_w.rearrange("(t p) k -> p t k", p=P)
        q_raw = [keep.tile([P, PACK, HW], BF16, name="q_raw%d" % b) for b in range(B)]
        cm_raw = [keep.tile([P, ROW_TILES, C], BF16, name="cm_raw%d" % b) for b in range(B)]
        w_raw = [keep.tile([P, PASSES * C], BF16, name="w_raw%d" % t) for t in range(OT)]

        def load_q(b):
            nc.sync.dma_start(out=q_raw[b][:], in_=q_view[:, b, :, :])

        def load_cm(b):
            nc.sync.dma_start(out=cm_raw[b][:], in_=cm_view[:, ROW_TILES * b : ROW_TILES * (b + 1), :])

        def load_w(t):
            nc.sync.dma_start(out=w_raw[t][:], in_=w_view[:, t, :])

        load_q(0)
        load_w(0)
        load_q(1)
        load_cm(0)
        load_q(2)
        load_q(4)
        load_cm(1)
        load_q(3)
        for b in range(2, B):
            load_cm(b)
        for t in range(1, OT):
            load_w(t)
        nc.sync.dma_start(out=gain_rows[0:OT, :], in_=bn_gamma.rearrange("(t p) -> t p", p=P))
        nc.sync.dma_start(out=gain_rows[OT : 2 * OT, :], in_=bn_beta.rearrange("(t p) -> t p", p=P))

        u_codes = keep.tile([P, PASSES, NPIX], U32, name="u_codes", align_bytes=64)
        u_scales = keep.tile([P, PASSES, NPIX], U8, name="u_scales", align_bytes=64)
        w_codes = keep.tile([P, OT, PASSES * P], U32, name="w_codes", align_bytes=64)
        w_scales = keep.tile([P, OT, PASSES * P], U8, name="w_scales", align_bytes=64)
        gram, above, q_rows, q_words = {}, {}, {}, {}
        squares = keep.tile([P, PACK, P], BF16, name="squares")
        q_t, sum_sq, inv_norm, inv_norm_all, q_grouped = {}, {}, {}, {}, {}
        cm_t, cm_grouped, w_t, w_grouped = {}, {}, {}, {}

        warm = prep_bank([P, BANK], "warm")
        for i in range(3):
            nc.tensor.matmul(out=warm[:, 0:P], lhsT=ident[:], rhs=ident[:], start=True, stop=True)

        def transpose_q(b):
            if b == B - 1:
                q_t[b] = psum.tile([P, PACK, P], F32, name="q_t%d" % b, tag="bank%d" % ROWS_BANK)
            else:
                q_t[b] = prep_bank([P, PACK, P], "q_t%d" % b)
            words = q_raw[b][:].bitcast(F32)
            for j in range(PACK):
                nc.tensor.transpose(q_t[b][:, j, :], words[:, j, :], ident[:])

        def norm_q(b):
            sum_sq[b] = keep.tile([P, PAIR], F32, name="sum_sq%d" % b)
            halves = q_t[b][:].bitcast(BF16).rearrange("m j (p e) -> m e j p", e=PAIR)
            for e in range(PAIR):
                nc.scalar.activation(
                    out=squares[:], in_=halves[:, e, :, :], func=ACT.Square, accum_out=sum_sq[b][:, e : e + 1]
                )

        def clamp_q(b):
            above[b] = keep.tile([P, PAIR], F32, name="above%d" % b)
            nc.scalar.activation(out=above[b][:], in_=sum_sq[b][:], func=ACT.Relu, bias=neg_l2_floor[:])

        def root_q(b):
            inv_norm[b] = keep.tile([P, PAIR], F32, name="inv_norm%d" % b)
            nc.scalar.activation(out=inv_norm[b][:], in_=above[b][:], func=ACT.Abs_reciprocal_sqrt, bias=l2_floor[:])

        def spread_norm(b):
            inv_norm_all[b] = prep_bank([P, BANK], "inv_norm_all%d" % b)
            for c in range(2):
                pixels = slice(c * P, (c + 1) * P) if b in GRAM else slice(c, HW, PAIR)
                nc.tensor.matmul(
                    out=inv_norm_all[b][:, pixels],
                    lhsT=inv_norm[b][:, c : c + 1].to_broadcast([P, P]),
                    rhs=ident[:],
                    start=True,
                    stop=True,
                    is_transpose=(b not in (0, 3)),
                )

        def gram_q(b):
            gram[b] = prep_bank([P, ROW_TILES, P], "gram%d" % b)
            for r in range(ROW_TILES):
                pixels = slice(r * P, (r + 1) * P)
                for j in range(PACK):
                    nc.tensor.matmul(
                        out=gram[b][:, r, :],
                        lhsT=q_raw[b][:, j, pixels],
                        rhs=q_raw[b][:, j, pixels],
                        start=(j == 0),
                        stop=False,
                    )
                nc.tensor.matmul(
                    out=gram[b][:, r, :], lhsT=ident_bf16[:], rhs=off_diagonal[:], start=False, stop=True
                )

        def norm_gram(b):
            above[b] = keep.tile([P, ROW_TILES], F32, name="above%d" % b)
            for r in range(ROW_TILES):
                nc.scalar.activation(
                    out=squares[:, r, :],
                    in_=gram[b][:, r, :],
                    func=ACT.Relu,
                    bias=neg_l2_floor[:],
                    accum_out=above[b][:, r : r + 1],
                )

        def scale_rows(b):
            q_rows[b] = keep.tile([P, PAIR, C], BF16, name="q_rows%d" % b)
            halves = q_t[b][:].bitcast(BF16).rearrange("m j (p e) -> m e p j", e=PAIR)
            for e in range(PAIR):
                nc.scalar.activation(
                    out=q_rows[b][:, e, :].rearrange("m (c i j) -> m c j i", i=RUN, j=PACK),
                    in_=halves[:, e, :, :].rearrange("m (c i) j -> m c j i", i=RUN),
                    func=ACT.Copy,
                    scale=inv_norm[b][:, e : e + 1],
                )

        def transpose_rows(b):
            q_words[b] = prep_bank([P, PAIR, PLANES, P], "q_words%d" % b)
            words = q_rows[b][:].bitcast(F32)
            for e in range(PAIR):
                for u in range(PLANES):
                    nc.tensor.transpose(q_words[b][:, e, u, :], words[:, e, u:WORDS:PLANES], ident[:])

        def copy_rows(b, copy):
            q_grouped[b] = keep.tile([P, HW, PACK], BF16, name="q_grouped%d" % b, align_bytes=64)
            copy(
                out=q_grouped[b][:].bitcast(F32).rearrange("p (m e) u -> p m e u", e=PAIR),
                in_=q_words[b][:].rearrange("p e u m -> p m e u"),
            )

        def normalise_q(b):
            q_grouped[b] = keep.tile([P, HW, PACK], BF16, name="q_grouped%d" % b, align_bytes=64)
            nc.vector.tensor_tensor(
                out=q_grouped[b][:].rearrange("p (c i) j -> p c j i", i=RUN),
                in0=inv_norm_all[b][:, 0:HW]
                .rearrange("p (c i) -> p c i", i=RUN)
                .unsqueeze(2)
                .to_broadcast([P, HW // RUN, PACK, RUN]),
                in1=q_raw[b][:].rearrange("p j (c i) -> p c j i", i=RUN),
                op=ALU.mult,
            )

        def quantise_q(b):
            pixels = slice(b * HW, (b + 1) * HW)
            nc.vector.quantize_mx(
                out=u_codes[:, 0, pixels].bitcast(FP8X4),
                scales=u_scales[:, 0, pixels],
                in_=q_grouped[b][:].rearrange("p x j -> p (x j)"),
            )

        def transpose_cm(b):
            cm_t[b] = prep_bank([P, ROW_TILES, PLANES, P], "cm_t%d" % b)
            words = cm_raw[b][:].bitcast(F32)
            for r in range(ROW_TILES):
                for u in range(PLANES):
                    nc.tensor.transpose(cm_t[b][:, r, u, :], words[:, r, u:WORDS:PLANES], ident[:])

        def copy_cm(b, copy):
            cm_grouped[b] = keep.tile([P, ROW_TILES, P, PACK], BF16, name="cm_grouped%d" % b, align_bytes=64)
            copy(out=cm_grouped[b][:].bitcast(F32), in_=cm_t[b][:].rearrange("p r u v -> p r v u"))

        def quantise_cm(b):
            pixels = slice(b * HW, (b + 1) * HW)
            nc.vector.quantize_mx(
                out=u_codes[:, 1, pixels].bitcast(FP8X4),
                scales=u_scales[:, 1, pixels],
                in_=cm_grouped[b][:].rearrange("p r v j -> p (r v j)"),
            )

        def transpose_w(t):
            w_t[t] = prep_bank([P, PASSES, PLANES, P], "w_t%d" % t)
            words = w_raw[t][:].bitcast(F32)
            for u in range(PLANES):
                nc.tensor.transpose(w_t[t][:, 0, u, :], words[:, u:WORDS:PLANES], ident[:])
            for u in range(PLANES):
                nc.tensor.transpose(w_t[t][:, 1, u, :], words[:, WORDS + u : 2 * WORDS : PLANES], ident[:])

        def copy_w(t, copy):
            w_grouped[t] = keep.tile([P, PASSES, P, PACK], BF16, name="w_grouped%d" % t, align_bytes=64)
            copy(out=w_grouped[t][:].bitcast(F32), in_=w_t[t][:].rearrange("p a u o -> p a o u"))

        def quantise_w(t):
            nc.vector.quantize_mx(
                out=w_codes[:, t, :].bitcast(FP8X4),
                scales=w_scales[:, t, :],
                in_=w_grouped[t][:].rearrange("p a o j -> p (a o j)"),
            )

        y, stats, mean_var, rstd, neg_mean_gamma, bn_scale, bn_shift = {}, {}, {}, {}, {}, {}, {}

        def multiply(t, i):
            first, n = CHUNKS[i]
            bank = Y_BANKS[(len(CHUNKS) * t + i) % BANKS]
            y[(t, i)] = psum.tile([P, BANK], F32, name="y%d_%d" % (t, i), tag="bank%d" % bank)
            for a in range(PASSES):
                nc.tensor.matmul_mx(
                    out=y[(t, i)][:, 0:n],
                    lhsT=w_codes[:, t, a * P : (a + 1) * P].bitcast(FP8X4),
                    lhsT_scale=w_scales[:, t, a * P : (a + 1) * P],
                    rhs=u_codes[:, a, first : first + n].bitcast(FP8X4),
                    rhs_scale=u_scales[:, a, first : first + n],
                    start=(a == 0),
                    stop=(a == PASSES - 1),
                )

        def chunk_statistics(t, i):
            if i == 0:
                stats[t] = keep.tile([P, len(CHUNKS), BN_STATS], F32, name="stats%d" % t)
            nc.vector.bn_stats(out=stats[t][:, i, :], in_=y[(t, i)][:, 0 : CHUNKS[i][1]])

        def statistics(t):
            for i in range(len(CHUNKS)):
                multiply(t, i)
                chunk_statistics(t, i)

        def aggregate(t):
            mean_var[t] = keep.tile([P, 2], F32, name="mean_var%d" % t)
            nc.vector.bn_aggr(out=mean_var[t][:], in_=stats[t][:].rearrange("p i s -> p (i s)"))

        def chain_first(t):
            rstd[t] = keep.tile([P, 1], F32, name="rstd%d" % t)
            nc.scalar.activation(
                out=rstd[t][:], in_=mean_var[t][:, 1:2], func=ACT.Abs_reciprocal_sqrt, bias=bn_eps[:]
            )
            neg_mean_gamma[t] = keep.tile([P, 1], F32, name="neg_mean_gamma%d" % t)
            nc.scalar.activation(
                out=neg_mean_gamma[t][:], in_=mean_var[t][:, 0:1], func=ACT.Copy, scale=neg_gamma[:, t : t + 1]
            )

        def chain_second(t):
            bn_scale[t] = keep.tile([P, 1], F32, name="bn_scale%d" % t)
            nc.scalar.activation(out=bn_scale[t][:], in_=rstd[t][:], func=ACT.Copy, scale=gain[:, t : t + 1])
            bn_shift[t] = keep.tile([P, 1], F32, name="bn_shift%d" % t)
            nc.scalar.activation(
                out=bn_shift[t][:],
                in_=rstd[t][:],
                func=ACT.Identity,
                scale=neg_mean_gamma[t][:],
                bias=gain[:, OT + t : OT + t + 1],
            )

        def store(t, first, n, result):
            nc.sync.dma_start(
                out=out[first // HW : (first + n) // HW, t * P : (t + 1) * P, :, :].rearrange("b p h w -> p b (h w)"),
                in_=result.rearrange("p (b x) -> p b x", x=HW),
            )

        def relu_scalar(t, i):
            first, n = CHUNKS[i]
            result = keep.tile([P, n], F32, name="result%d_%d" % (t, i))
            nc.scalar.activation(
                out=result[:], in_=y[(t, i)][:, 0:n], func=ACT.Relu, bias=bn_shift[t][:], scale=bn_scale[t][:]
            )
            store(t, first, n, result[:])

        def relu_vector(t, i):
            first, n = CHUNKS[i]
            result = keep.tile([P, n], F32, name="result%d_%d" % (t, i))
            for x0 in range(0, n, HW):
                nc.vector.tensor_scalar(
                    out=result[:, x0 : x0 + HW],
                    in0=y[(t, i)][:, x0 : x0 + HW],
                    scalar1=bn_scale[t][:],
                    scalar2=bn_shift[t][:],
                    op0=ALU.mult,
                    op1=ALU.add,
                )
            for x0 in range(0, n, HW):
                nc.vector.tensor_scalar(
                    out=result[:, x0 : x0 + HW], in0=result[:, x0 : x0 + HW], scalar1=0.0, scalar2=None, op0=ALU.max
                )
                store(t, first + x0, HW, result[:, x0 : x0 + HW])

        transpose_q(0)
        transpose_w(0)
        transpose_q(1)
        transpose_cm(0)
        norm_q(0)
        clamp_q(0)
        root_q(0)
        copy_w(0, nc.vector.tensor_copy)
        copy_cm(0, nc.vector.tensor_copy)
        norm_q(1)
        gram_q(2)
        quantise_w(0)
        spread_norm(0)
        transpose_q(4)
        normalise_q(0)
        quantise_cm(0)
        norm_gram(2)
        clamp_q(1)
        root_q(2)
        root_q(1)
        transpose_cm(1)
        spread_norm(1)
        norm_q(4)
        normalise_q(1)
        quantise_q(0)
        spread_norm(2)
        gram_q(3)
        normalise_q(2)
        copy_cm(1, nc.scalar.copy)
        norm_gram(3)
        clamp_q(4)
        root_q(3)
        root_q(4)
        transpose_cm(2)
        transpose_cm(3)
        spread_norm(3)
        copy_cm(2, nc.scalar.copy)
        quantise_q(1)
        quantise_cm(1)
        quantise_q(2)
        normalise_q(3)
        transpose_cm(4)
        gain_t = prep_bank([P, 2 * BANK], "gain_t", BF16)
        nc.tensor.transpose(gain_t[:, 0:P], gain_rows[:], ident_bf16[:])
        transpose_w(1)
        scale_rows(4)
        copy_cm(3, nc.scalar.copy)
        copy_cm(4, nc.scalar.copy)
        transpose_rows(4)
        multiply(0, 0)
        quantise_cm(2)
        quantise_q(3)
        quantise_cm(3)
        quantise_cm(4)
        multiply(0, 1)
        transpose_w(2)
        transpose_w(3)
        copy_rows(4, nc.scalar.copy)
        quantise_q(4)
        multiply(0, 2)
        chunk_statistics(0, 0)
        copy_w(1, nc.scalar.copy)
        gain = keep.tile([P, 2 * OT], F32, name="gain")
        nc.scalar.copy(out=gain[:], in_=gain_t[:, 0 : 2 * OT])
        neg_gamma = keep.tile([P, OT], F32, name="neg_gamma")
        nc.scalar.activation(out=neg_gamma[:], in_=gain_t[:, 0:OT], func=ACT.Copy, scale=-1.0)
        copy_w(2, nc.scalar.copy)
        quantise_w(1)
        chunk_statistics(0, 1)
        chunk_statistics(0, 2)
        quantise_w(2)
        aggregate(0)
        copy_w(3, nc.scalar.copy)
        chain_first(0)
        chain_second(0)
        statistics(1)
        quantise_w(3)
        aggregate(1)
        for t in range(OT):
            for i in range(len(CHUNKS)):
                if i == len(CHUNKS) - 1 and t + 1 < OT:
                    chain_first(t + 1)
                if (t, i) in VECTOR_RELU:
                    relu_vector(t, i)
                else:
                    relu_scalar(t, i)
            if t + 1 < OT:
                chain_second(t + 1)
            if t + 2 < OT:
                statistics(t + 2)
                aggregate(t + 2)
